import numpy as np
import ml_dtypes


def mxq(x, axis, fmt="e4m3"):
    dtype, down = {"e4m3": (ml_dtypes.float8_e4m3fn, 7), "e5m2": (ml_dtypes.float8_e5m2, 14)}[fmt]
    v = np.moveaxis(np.asarray(x, np.float32).astype(ml_dtypes.bfloat16).astype(np.float64), axis, -1)
    blocks = v.reshape(v.shape[:-1] + (-1, 32))
    amax = np.abs(blocks).max(-1, keepdims=True)
    byte = np.maximum(np.where(amax > 0, np.frexp(amax)[1] - 1 + 127, 0) - down, 1)
    scale = np.exp2(byte - 127.0)
    codes = (blocks / scale).astype(np.float32).astype(dtype).astype(np.float64)
    return np.moveaxis((codes * scale).reshape(v.shape), -1, axis)


WIDE = False


def mx_kscale(k):
    if not WIDE:
        return np.ones(k)
    levels = np.array([10, -10, 5, -5, 0])
    a = np.random.permutation(np.resize(levels, k // 512 * 4)).reshape(k // 512, 4)
    idx = np.arange(k)
    return np.exp2(a[idx // 512, idx % 128 // 32])


BF16 = ml_dtypes.bfloat16


def bf(x):
    return np.asarray(x, np.float32).astype(BF16)


def f64(x):
    return np.asarray(x).astype(np.float64)


B, N, D, H = 128, 17, 2048, 32
D2 = D // 2
D4 = D // 4
EPS = 1e-5


def layernorm(z, g, b):
    mu = z.mean(-1, keepdims=True)
    var = z.var(-1, keepdims=True)
    return (z - mu) / np.sqrt(var + EPS) * g + b


def setup_inputs():
    s, t = mx_kscale(D), mx_kscale(D2)
    r = np.random.standard_normal
    return {"query": bf(r((B, N, D)) * s),
            "A1W": bf(r((D, D2)) / np.sqrt(D) / s[:, None]),
            "A1b": bf(r(D2) * 0.2),
            "g1": bf((1.0 + 0.1 * r(D2)) * t),
            "b1": bf(r(D2) * 0.2 * t),
            "A2W": bf(r((D2, D4)) / np.sqrt(D2) / t[:, None]),
            "A2b": bf(r(D4) * 0.2),
            "g2": bf(1.0 + 0.1 * r(D4)),
            "b2": bf(r(D4) * 0.2)}


def reference(query, A1W, A1b, g1, b1, A2W, A2b, g2, b2):
    u = (mxq(f64(query), 2, "e4m3") @ mxq(f64(A1W), 0, "e4m3")) + f64(A1b)
    j1 = np.maximum(layernorm(u, f64(g1), f64(b1)), 0.0)
    w = (mxq(j1, 2, "e4m3") @ mxq(f64(A2W), 0, "e4m3")) + f64(A2b)
    return np.maximum(layernorm(w, f64(g2), f64(b2)), 0.0)

@@ -1,0 +1,375 @@
+from contextlib import ExitStack
+
+import concourse.mybir as mybir
+from concourse.masks import make_identity
+
+F32 = mybir.dt.float32
+BF16 = mybir.dt.bfloat16
+U32 = mybir.dt.uint32
+U8 = mybir.dt.uint8
+FP8X4 = mybir.dt.float8_e4m3fn_x4
+ALU = mybir.AluOpType
+ACT = mybir.ActivationFunctionType
+
+P = 128
+PACK = 4
+K_PASS = P * PACK
+BANK = 512
+
+TOKENS = 128 * 17
+D = 2048
+D2 = 1024
+D4 = 512
+EPS = 1e-5
+TILES = TOKENS // P
+PASSES1 = D // K_PASS
+PASSES2 = D2 // K_PASS
+HALVES1 = D2 // BANK
+
+FLOPS = 2 * TOKENS * (D * D2 + D2 * D4)
+
+W1_LEAD = 5
+TQ_LEAD = 3
+Q_LEAD = 2
+MX1_LEAD = 1
+Q_BUFS = 8
+
+
+def tile_multiheadedattention_pa_kernel(tc, query, A1W, A1b, g1, b1, A2W, A2b, g2, b2, out):
+    nc = tc.nc
+    q_rows = query.flatten_outer_dims()
+    out_rows = out.flatten_outer_dims()
+    w1_view = A1W.rearrange("(g u p e) n -> g p u (e n)", g=PASSES1, u=2, p=P, e=2)
+    w2_view = A2W.rearrange("(c t p) n -> c p t n", c=PASSES2, t=PACK, p=P)
+
+    with ExitStack() as ctx:
+        keep = ctx.enter_context(tc.tile_pool(name="keep", bufs=1))
+        q_pool = ctx.enter_context(tc.tile_pool(name="q_pool", bufs=Q_BUFS))
+        w_pool = ctx.enter_context(tc.tile_pool(name="w_pool", bufs=2))
+        work = ctx.enter_context(tc.tile_pool(name="work", bufs=2))
+        small = ctx.enter_context(tc.tile_pool(name="small", bufs=4))
+        psum = ctx.enter_context(tc.psum_pool(name="psum", bufs=2))
+        ctx.enter_context(tc.manual_schedule())
+
+        ident = keep.tile([P, P], F32)
+        make_identity(nc, ident[:])
+        eps = keep.tile([P, 1], F32)
+        nc.vector.memset(eps[:], EPS)
+        table_warm = keep.tile([P, 1], F32)
+        nc.scalar.activation(out=table_warm[:], in_=eps[:], func=ACT.Sqrt)
+
+        gb_rows = keep.tile([2 * D2 // P, P], BF16)
+        nc.scalar.dma_start(out=gb_rows[0 : D2 // P, :], in_=g1.rearrange("(j p) -> j p", p=P))
+        nc.scalar.dma_start(out=gb_rows[D2 // P : 2 * D2 // P, :], in_=b1.rearrange("(j p) -> j p", p=P))
+
+        q_tiles = {}
+        w1_raw = {}
+        w2_raw = {}
+
+        def load_query(i):
+            q_sb = q_pool.tile([P, D], BF16)
+            nc.sync.dma_start(out=q_sb[:], in_=q_rows[i * P : (i + 1) * P, :])
+            q_tiles[i] = q_sb
+
+        def load_w1(g):
+            raw1 = keep.tile([P, 2, 2 * D2], BF16, name="raw1_%d" % g)
+            nc.sync.dma_start(out=raw1[:], in_=w1_view[g])
+            w1_raw[g] = raw1
+
+        def load_w2(c):
+            raw2 = keep.tile([P, PACK, D4], BF16, name="raw2_%d" % c)
+            nc.sync.dma_start(out=raw2[:], in_=w2_view[c])
+            w2_raw[c] = raw2
+
+        def load_row_to_all_partitions(vec, width, name):
+            spread = keep.tile([P, width], BF16, name=name)
+            nc.sync.dma_start(out=spread[:], in_=vec.partition_broadcast(P))
+            return spread
+
+        load_w1(0)
+        load_w1(1)
+        load_query(0)
+        load_w1(2)
+        load_w1(3)
+        a1_all = load_row_to_all_partitions(A1b, D2, "a1_all")
+        load_query(1)
+        load_query(2)
+        load_w2(0)
+        load_w2(1)
+        a2_all = load_row_to_all_partitions(A2b, D4, "a2_all")
+        g2_all = load_row_to_all_partitions(g2, D4, "g2_all")
+        b2_all = load_row_to_all_partitions(b2, D4, "b2_all")
+        for i in range(3, Q_BUFS):
+            load_query(i)
+
+        gb_square = keep.tile([P, P], F32)
+        nc.vector.memset(gb_square[:], 0.0)
+        nc.vector.tensor_copy(out=gb_square[0 : 2 * D2 // P, :], in_=gb_rows[:])
+        gb_t = psum.tile([P, P], F32, tag="acc2", bufs=1)
+        nc.tensor.transpose(gb_t[:], gb_square[:], ident[:])
+        gb = keep.tile([P, 2 * D2 // P], F32)
+        nc.vector.tensor_copy(out=gb[:], in_=gb_t[:, 0 : 2 * D2 // P])
+
+        w1_codes = keep.tile([P, PASSES1, D2], U32, align_bytes=64)
+        w1_scales = keep.tile([P, PASSES1, D2], U8, align_bytes=64)
+        w2_codes = keep.tile([P, PASSES2, D4], U32, align_bytes=64)
+        w2_scales = keep.tile([P, PASSES2, D4], U8, align_bytes=64)
+        w2_grouped = {}
+
+        def regroup(copy, dst, src):
+            copy(
+                out=dst.rearrange("p (c i) t -> p c t i", i=4),
+                in_=src.rearrange("p t (c i) -> p c t i", i=4),
+            )
+
+        def prepare_w1(g):
+            rows = w1_raw[g][:].rearrange("p u (e n) -> p (u e) n", e=2)
+            by_scalar = w_pool.tile([P, BANK, PACK], BF16, align_bytes=64)
+            regroup(nc.scalar.copy, by_scalar[:], rows[:, :, BANK : 2 * BANK])
+            by_vector = w_pool.tile([P, BANK, PACK], BF16, align_bytes=64)
+            regroup(nc.vector.tensor_copy, by_vector[:], rows[:, :, 0:BANK])
+            for h, grouped in enumerate((by_vector, by_scalar)):
+                cols = slice(h * BANK, (h + 1) * BANK)
+                nc.vector.quantize_mx(
+                    out=w1_codes[:, g, cols].bitcast(FP8X4),
+                    scales=w1_scales[:, g, cols],
+                    in_=grouped[:].rearrange("p n t -> p (n t)"),
+                )
+
+        def regroup_w2(c):
+            grouped2 = keep.tile([P, D4, PACK], BF16, align_bytes=64, name="grouped2_%d" % c)
+            regroup(nc.scalar.copy, grouped2[:], w2_raw[c][:])
+            w2_grouped[c] = grouped2
+
+        def quantise_w2(c):
+            nc.vector.quantize_mx(
+                out=w2_codes[:, c, :].bitcast(FP8X4),
+                scales=w2_scales[:, c, :],
+                in_=w2_grouped[c][:].rearrange("p n t -> p (n t)"),
+            )
+
+        q_banks = {}
+        q_grouped = {}
+        q_codes = {}
+        q_scales = {}
+        u_banks = {}
+        u_tiles = {}
+        stats1 = {}
+        z_tiles = {}
+        z_banks = {}
+        j_planes = {}
+        j_grouped = {}
+        j_codes = {}
+        j_scales = {}
+        w_banks = {}
+        w_tiles = {}
+        stats2 = {}
+        y_tiles = {}
+
+        def transpose_query(i):
+            words = q_tiles[i][:].bitcast(F32)
+            q_banks[i] = []
+            for b in range(2):
+                qt = psum.tile([P, 2, 2, P], F32)
+                for gg in range(2):
+                    for u in range(2):
+                        first = 256 * (2 * b + gg) + P * u
+                        nc.tensor.transpose(qt[:, gg, u, :], words[:, first : first + P], ident[:])
+                q_banks[i].append(qt)
+
+        def query_out_of_psum(i):
+            qg = work.tile([P, PASSES1 * P * PACK], BF16, align_bytes=64)
+            qg_words = qg[:].bitcast(F32).rearrange("p (g n u) -> p g n u", g=PASSES1, u=2)
+            for b in range(2):
+                nc.scalar.copy(
+                    out=qg_words[:, 2 * b : 2 * b + 2, :, :],
+                    in_=q_banks[i][b][:].rearrange("p g u n -> p g n u"),
+                )
+            q_grouped[i] = qg
+
+        def quantise_query(i):
+            qc = work.tile([P, PASSES1 * P], U32, align_bytes=64)
+            qs = work.tile([P, PASSES1 * P], U8, align_bytes=64)
+            nc.vector.quantize_mx(out=qc[:].bitcast(FP8X4), scales=qs[:], in_=q_grouped[i][:])
+            q_codes[i] = qc
+            q_scales[i] = qs
+
+        def first_product(i):
+            u_banks[i] = []
+            for h in range(HALVES1):
+                cols = slice(h * BANK, (h + 1) * BANK)
+                acc1 = psum.tile([P, BANK], F32)
+                for g in range(PASSES1):
+                    toks = slice(g * P, (g + 1) * P)
+                    nc.tensor.matmul_mx(
+                        out=acc1[:],
+                        lhsT=q_codes[i][:, toks].bitcast(FP8X4),
+                        lhsT_scale=q_scales[i][:, toks],
+                        rhs=w1_codes[:, g, cols].bitcast(FP8X4),
+                        rhs_scale=w1_scales[:, g, cols],
+                        start=(g == 0),
+                        stop=(g == PASSES1 - 1),
+                    )
+                u_banks[i].append(acc1)
+
+        def add_bias1(i):
+            u = work.tile([P, D2], F32)
+            row_sum = small.tile([P, HALVES1], F32)
+            for h in range(HALVES1):
+                cols = slice(h * BANK, (h + 1) * BANK)
+                nc.vector.scalar_tensor_tensor(
+                    out=u[:, cols], in0=u_banks[i][h][:], scalar=1.0, in1=a1_all[:, cols],
+                    op0=ALU.mult, op1=ALU.add, accum_out=row_sum[:, h : h + 1],
+                )
+            neg_mean = small.tile([P, 1], F32)
+            nc.vector.tensor_scalar(
+                out=neg_mean[:], in0=row_sum[:, 0:1], scalar1=row_sum[:, 1:2], scalar2=-1.0 / D2,
+                op0=ALU.add, op1=ALU.mult,
+            )
+            u_tiles[i] = u
+            stats1[i] = {"neg_mean": neg_mean}
+
+        def deviation1(i):
+            squares = work.tile([P, D2], F32)
+            sq_sum = small.tile([P, 1], F32)
+            nc.scalar.activation(
+                out=squares[:], in_=u_tiles[i][:], func=ACT.Square,
+                bias=stats1[i]["neg_mean"][:], scale=1.0, accum_out=sq_sum[:],
+            )
+            std = small.tile([P, 1], F32)
+            nc.scalar.activation(out=std[:], in_=sq_sum[:], func=ACT.Sqrt, bias=eps[:], scale=1.0 / D2)
+            stats1[i]["std"] = std
+
+        def normalise1(i):
+            rstd = small.tile([P, 1], F32)
+            nc.vector.reciprocal(out=rstd[:], in_=stats1[i]["std"][:])
+            z = work.tile([P, D2], F32)
+            nc.vector.tensor_scalar(
+                out=z[:], in0=u_tiles[i][:], scalar1=stats1[i]["neg_mean"][:], scalar2=rstd[:],
+                op0=ALU.add, op1=ALU.mult,
+            )
+            z_tiles[i] = z
+
+        def transpose_z(i):
+            z_banks[i] = []
+            for c in range(PASSES2):
+                zt = psum.tile([P, PACK, P], F32)
+                for t in range(PACK):
+                    first = K_PASS * c + P * t
+                    nc.tensor.transpose(zt[:, t, :], z_tiles[i][:, first : first + P], ident[:])
+                z_banks[i].append(zt)
+
+        def gain_shift_relu1(i):
+            planes = work.tile([P, PASSES2, PACK, P], BF16)
+            for c in range(PASSES2):
+                for t in range(PACK):
+                    j = PACK * c + t
+                    nc.scalar.activation(
+                        out=planes[:, c, t, :], in_=z_banks[i][c][:, t, :], func=ACT.Relu,
+                        scale=gb[:, j : j + 1], bias=gb[:, D2 // P + j : D2 // P + j + 1],
+                    )
+            j_planes[i] = planes
+
+        def regroup_j1(i):
+            jg = work.tile([P, PASSES2, P, PACK], BF16, align_bytes=64)
+            nc.vector.tensor_copy(out=jg[:], in_=j_planes[i][:].rearrange("p c t n -> p c n t"))
+            j_grouped[i] = jg
+
+        def quantise_j1(i):
+            jc = work.tile([P, PASSES2 * P], U32, align_bytes=64)
+            js = work.tile([P, PASSES2 * P], U8, align_bytes=64)
+            nc.vector.quantize_mx(
+                out=jc[:].bitcast(FP8X4), scales=js[:],
+                in_=j_grouped[i][:].rearrange("p c n t -> p (c n t)"),
+            )
+            j_codes[i] = jc
+            j_scales[i] = js
+
+        def second_product(i):
+            acc2 = psum.tile([P, BANK], F32, bufs=1)
+            for c in range(PASSES2):
+                toks = slice(c * P, (c + 1) * P)
+                nc.tensor.matmul_mx(
+                    out=acc2[:],
+                    lhsT=j_codes[i][:, toks].bitcast(FP8X4),
+                    lhsT_scale=j_scales[i][:, toks],
+                    rhs=w2_codes[:, c, :].bitcast(FP8X4),
+                    rhs_scale=w2_scales[:, c, :],
+                    start=(c == 0),
+                    stop=(c == PASSES2 - 1),
+                )
+            w_banks[i] = acc2
+
+        def add_bias2(i):
+            w = work.tile([P, D4], F32, bufs=3)
+            row_sum2 = small.tile([P, 1], F32)
+            nc.vector.scalar_tensor_tensor(
+                out=w[:], in0=w_banks[i][:], scalar=1.0, in1=a2_all[:],
+                op0=ALU.mult, op1=ALU.add, accum_out=row_sum2[:],
+            )
+            neg_mean2 = small.tile([P, 1], F32)
+            nc.vector.tensor_scalar(
+                out=neg_mean2[:], in0=row_sum2[:], scalar1=-1.0 / D4, scalar2=None, op0=ALU.mult,
+            )
+            w_tiles[i] = w
+            stats2[i] = {"neg_mean": neg_mean2}
+
+        def deviation2(i):
+            squares2 = work.tile([P, D4], F32)
+            sq_sum2 = small.tile([P, 1], F32)
+            nc.scalar.activation(
+                out=squares2[:], in_=w_tiles[i][:], func=ACT.Square,
+                bias=stats2[i]["neg_mean"][:], scale=1.0, accum_out=sq_sum2[:],
+            )
+            std2 = small.tile([P, 1], F32)
+            nc.scalar.activation(out=std2[:], in_=sq_sum2[:], func=ACT.Sqrt, bias=eps[:], scale=1.0 / D4)
+            stats2[i]["std"] = std2
+
+        def norm_gain_shift2(i):
+            rstd2 = small.tile([P, 1], F32)
+            nc.vector.reciprocal(out=rstd2[:], in_=stats2[i]["std"][:])
+            x = work.tile([P, D4], F32)
+            nc.vector.scalar_tensor_tensor(
+                out=x[:], in0=w_tiles[i][:], scalar=stats2[i]["neg_mean"][:], in1=g2_all[:],
+                op0=ALU.add, op1=ALU.mult,
+            )
+            y = work.tile([P, D4], F32)
+            nc.vector.scalar_tensor_tensor(
+                out=y[:], in0=x[:], scalar=rstd2[:], in1=b2_all[:], op0=ALU.mult, op1=ALU.add,
+            )
+            y_tiles[i] = y
+
+        def relu_and_store(i):
+            result = work.tile([P, D4], F32, bufs=3)
+            nc.scalar.activation(out=result[:], in_=y_tiles[i][:], func=ACT.Relu)
+            nc.sync.dma_start(out=out_rows[i * P : (i + 1) * P, :], in_=result[:])
+
+        def run(step, i):
+            if 0 <= i < TILES:
+                step(i)
+
+        for i in range(-W1_LEAD, TILES + 3):
+            if Q_BUFS <= i + TQ_LEAD - 1 + Q_BUFS < TILES:
+                load_query(i + TQ_LEAD - 1 + Q_BUFS)
+            run(add_bias1, i)
+            run(query_out_of_psum, i + Q_LEAD)
+            run(first_product, i + MX1_LEAD)
+            run(regroup_j1, i - 1)
+            run(deviation1, i)
+            run(quantise_query, i + Q_LEAD)
+            if 0 <= i < PASSES2:
+                quantise_w2(i)
+            run(quantise_j1, i - 1)
+            run(second_product, i - 1)
+            run(normalise1, i)
+            run(relu_and_store, i - 3)
+            run(deviation2, i - 2)
+            run(transpose_z, i)
+            run(transpose_query, i + TQ_LEAD)
+            run(add_bias2, i - 1)
+            run(norm_gain_shift2, i - 2)
+            run(gain_shift_relu1, i)
+            if 0 <= i + W1_LEAD < PASSES1:
+                prepare_w1(i + W1_LEAD)
+            if 0 <= i + 1 < PASSES2:
+                regroup_w2(i + 1)

@@ -28,10 +28,6 @@ HALVES1 = D2 // BANK
 
 FLOPS = 2 * TOKENS * (D * D2 + D2 * D4)
 
-W1_LEAD = 5
-TQ_LEAD = 3
-Q_LEAD = 2
-MX1_LEAD = 1
 Q_BUFS = 8
 
 
@@ -56,11 +52,11 @@ def tile_multiheadedattention_pa_kernel(tc, query, A1W, A1b, g1, b1, A2W, A2b, g
         eps = keep.tile([P, 1], F32)
         nc.vector.memset(eps[:], EPS)
         table_warm = keep.tile([P, 1], F32)
-        nc.scalar.activation(out=table_warm[:], in_=eps[:], func=ACT.Sqrt)
+        nc.scalar.activation(out=table_warm[:], in_=eps[:], func=ACT.Abs_reciprocal_sqrt)
 
         gb_rows = keep.tile([2 * D2 // P, P], BF16)
-        nc.scalar.dma_start(out=gb_rows[0 : D2 // P, :], in_=g1.rearrange("(j p) -> j p", p=P))
-        nc.scalar.dma_start(out=gb_rows[D2 // P : 2 * D2 // P, :], in_=b1.rearrange("(j p) -> j p", p=P))
+        nc.sync.dma_start(out=gb_rows[0 : D2 // P, :], in_=g1.rearrange("(j p) -> j p", p=P))
+        nc.sync.dma_start(out=gb_rows[D2 // P : 2 * D2 // P, :], in_=b1.rearrange("(j p) -> j p", p=P))
 
         q_tiles = {}
         w1_raw = {}
@@ -105,7 +101,7 @@ def tile_multiheadedattention_pa_kernel(tc, query, A1W, A1b, g1, b1, A2W, A2b, g
         gb_square = keep.tile([P, P], F32)
         nc.vector.memset(gb_square[:], 0.0)
         nc.vector.tensor_copy(out=gb_square[0 : 2 * D2 // P, :], in_=gb_rows[:])
-        gb_t = psum.tile([P, P], F32, tag="acc2", bufs=1)
+        gb_t = psum.tile([P, P], F32, tag="acc2")
         nc.tensor.transpose(gb_t[:], gb_square[:], ident[:])
         gb = keep.tile([P, 2 * D2 // P], F32)
         nc.vector.tensor_copy(out=gb[:], in_=gb_t[:, 0 : 2 * D2 // P])
@@ -122,19 +118,29 @@ def tile_multiheadedattention_pa_kernel(tc, query, A1W, A1b, g1, b1, A2W, A2b, g
                 in_=src.rearrange("p t (c i) -> p c t i", i=4),
             )
 
-        def prepare_w1(g):
+        w1_grouped = {}
+
+        def regroup_w1(g):
             rows = w1_raw[g][:].rearrange("p u (e n) -> p (u e) n", e=2)
             by_scalar = w_pool.tile([P, BANK, PACK], BF16, align_bytes=64)
             regroup(nc.scalar.copy, by_scalar[:], rows[:, :, BANK : 2 * BANK])
             by_vector = w_pool.tile([P, BANK, PACK], BF16, align_bytes=64)
             regroup(nc.vector.tensor_copy, by_vector[:], rows[:, :, 0:BANK])
-            for h, grouped in enumerate((by_vector, by_scalar)):
-                cols = slice(h * BANK, (h + 1) * BANK)
-                nc.vector.quantize_mx(
-                    out=w1_codes[:, g, cols].bitcast(FP8X4),
-                    scales=w1_scales[:, g, cols],
-                    in_=grouped[:].rearrange("p n t -> p (n t)"),
-                )
+            w1_grouped[g] = (by_vector, by_scalar)
+
+        def quantise_w1(g, h):
+            cols = slice(h * BANK, (h + 1) * BANK)
+            nc.vector.quantize_mx(
+                out=w1_codes[:, g, cols].bitcast(FP8X4),
+                scales=w1_scales[:, g, cols],
+                in_=w1_grouped[g][h][:].rearrange("p n t -> p (n t)"),
+            )
+
+        def prepare_w1(g):
+            regroup_w1(g)
+            if g > 0:
+                quantise_w1(g - 1, 1)
+            quantise_w1(g, 0)
 
         def regroup_w2(c):
             grouped2 = keep.tile([P, D4, PACK], BF16, align_bytes=64, name="grouped2_%d" % c)
@@ -236,16 +242,16 @@ def tile_multiheadedattention_pa_kernel(tc, query, A1W, A1b, g1, b1, A2W, A2b, g
                 out=squares[:], in_=u_tiles[i][:], func=ACT.Square,
                 bias=stats1[i]["neg_mean"][:], scale=1.0, accum_out=sq_sum[:],
             )
-            std = small.tile([P, 1], F32)
-            nc.scalar.activation(out=std[:], in_=sq_sum[:], func=ACT.Sqrt, bias=eps[:], scale=1.0 / D2)
-            stats1[i]["std"] = std
+            rstd = small.tile([P, 1], F32)
+            nc.scalar.activation(
+                out=rstd[:], in_=sq_sum[:], func=ACT.Abs_reciprocal_sqrt, bias=eps[:], scale=1.0 / D2,
+            )
+            stats1[i]["rstd"] = rstd
 
         def normalise1(i):
-            rstd = small.tile([P, 1], F32)
-            nc.vector.reciprocal(out=rstd[:], in_=stats1[i]["std"][:])
             z = work.tile([P, D2], F32)
             nc.vector.tensor_scalar(
-                out=z[:], in0=u_tiles[i][:], scalar1=stats1[i]["neg_mean"][:], scalar2=rstd[:],
+                out=z[:], in0=u_tiles[i][:], scalar1=stats1[i]["neg_mean"][:], scalar2=stats1[i]["rstd"][:],
                 op0=ALU.add, op1=ALU.mult,
             )
             z_tiles[i] = z
@@ -286,7 +292,7 @@ def tile_multiheadedattention_pa_kernel(tc, query, A1W, A1b, g1, b1, A2W, A2b, g
             j_scales[i] = js
 
         def second_product(i):
-            acc2 = psum.tile([P, BANK], F32, bufs=1)
+            acc2 = psum.tile([P, BANK], F32)
             for c in range(PASSES2):
                 toks = slice(c * P, (c + 1) * P)
                 nc.tensor.matmul_mx(
@@ -321,55 +327,69 @@ def tile_multiheadedattention_pa_kernel(tc, query, A1W, A1b, g1, b1, A2W, A2b, g
                 out=squares2[:], in_=w_tiles[i][:], func=ACT.Square,
                 bias=stats2[i]["neg_mean"][:], scale=1.0, accum_out=sq_sum2[:],
             )
-            std2 = small.tile([P, 1], F32)
-            nc.scalar.activation(out=std2[:], in_=sq_sum2[:], func=ACT.Sqrt, bias=eps[:], scale=1.0 / D4)
-            stats2[i]["std"] = std2
-
-        def norm_gain_shift2(i):
             rstd2 = small.tile([P, 1], F32)
-            nc.vector.reciprocal(out=rstd2[:], in_=stats2[i]["std"][:])
+            nc.scalar.activation(
+                out=rstd2[:], in_=sq_sum2[:], func=ACT.Abs_reciprocal_sqrt, bias=eps[:], scale=1.0 / D4,
+            )
+            stats2[i]["rstd"] = rstd2
+
+        x_tiles = {}
+
+        def centre_gain2(i):
             x = work.tile([P, D4], F32)
             nc.vector.scalar_tensor_tensor(
                 out=x[:], in0=w_tiles[i][:], scalar=stats2[i]["neg_mean"][:], in1=g2_all[:],
                 op0=ALU.add, op1=ALU.mult,
             )
+            x_tiles[i] = x
+
+        def scale_shift2(i):
             y = work.tile([P, D4], F32)
             nc.vector.scalar_tensor_tensor(
-                out=y[:], in0=x[:], scalar=rstd2[:], in1=b2_all[:], op0=ALU.mult, op1=ALU.add,
+                out=y[:], in0=x_tiles[i][:], scalar=stats2[i]["rstd"][:], in1=b2_all[:],
+                op0=ALU.mult, op1=ALU.add,
             )
             y_tiles[i] = y
 
         def relu_and_store(i):
             result = work.tile([P, D4], F32, bufs=3)
-            nc.scalar.activation(out=result[:], in_=y_tiles[i][:], func=ACT.Relu)
+            nc.vector.tensor_scalar_max(out=result[:], in0=y_tiles[i][:], scalar1=0.0)
             nc.sync.dma_start(out=out_rows[i * P : (i + 1) * P, :], in_=result[:])
 
         def run(step, i):
             if 0 <= i < TILES:
                 step(i)
 
-        for i in range(-W1_LEAD, TILES + 3):
-            if Q_BUFS <= i + TQ_LEAD - 1 + Q_BUFS < TILES:
-                load_query(i + TQ_LEAD - 1 + Q_BUFS)
-            run(add_bias1, i)
-            run(query_out_of_psum, i + Q_LEAD)
-            run(first_product, i + MX1_LEAD)
-            run(regroup_j1, i - 1)
-            run(deviation1, i)
-            run(quantise_query, i + Q_LEAD)
+        def period(i):
+            if Q_BUFS <= i + Q_BUFS < TILES:
+                load_query(i + Q_BUFS)
+            run(transpose_z, i - 2)
+            run(transpose_query, i + 1)
+            run(regroup_j1, i - 3)
+            run(quantise_query, i)
+            if 0 <= i - 1 < PASSES2:
+                quantise_w2(i - 1)
+            run(quantise_j1, i - 3)
+            run(deviation2, i - 4)
+            run(deviation1, i - 1)
+            run(first_product, i)
+            run(second_product, i - 3)
+            run(centre_gain2, i - 4)
+            run(relu_and_store, i - 5)
+            run(scale_shift2, i - 4)
+            run(normalise1, i - 1)
+            run(query_out_of_psum, i + 1)
+            run(gain_shift_relu1, i - 2)
             if 0 <= i < PASSES2:
-                quantise_w2(i)
-            run(quantise_j1, i - 1)
-            run(second_product, i - 1)
-            run(normalise1, i)
-            run(relu_and_store, i - 3)
-            run(deviation2, i - 2)
-            run(transpose_z, i)
-            run(transpose_query, i + TQ_LEAD)
-            run(add_bias2, i - 1)
-            run(norm_gain_shift2, i - 2)
-            run(gain_shift_relu1, i)
-            if 0 <= i + W1_LEAD < PASSES1:
-                prepare_w1(i + W1_LEAD)
-            if 0 <= i + 1 < PASSES2:
-                regroup_w2(i + 1)
+                regroup_w2(i)
+            run(add_bias1, i)
+            run(add_bias2, i - 3)
+
+        prepare_w1(0)
+        prepare_w1(1)
+        period(-1)
+        prepare_w1(2)
+        prepare_w1(3)
+        quantise_w1(PASSES1 - 1, 1)
+        for i in range(TILES + 5):
+            period(i)

@@ -25,6 +25,7 @@ TILES = TOKENS // P
 PASSES1 = D // K_PASS
 PASSES2 = D2 // K_PASS
 HALVES1 = D2 // BANK
+PAIRS = (TILES + 1) // 2
 
 FLOPS = 2 * TOKENS * (D * D2 + D2 * D4)
 
@@ -249,56 +250,72 @@ def tile_multiheadedattention_pa_kernel(tc, query, A1W, A1b, g1, b1, A2W, A2b, g
             stats1[i]["rstd"] = rstd
 
         def normalise1(i):
-            z = work.tile([P, D2], F32)
+            z = work.tile([P, D2], F32, bufs=4)
             nc.vector.tensor_scalar(
                 out=z[:], in0=u_tiles[i][:], scalar1=stats1[i]["neg_mean"][:], scalar2=stats1[i]["rstd"][:],
                 op0=ALU.add, op1=ALU.mult,
             )
             z_tiles[i] = z
 
-        def transpose_z(i):
-            z_banks[i] = []
-            for c in range(PASSES2):
-                zt = psum.tile([P, PACK, P], F32)
-                for t in range(PACK):
-                    first = K_PASS * c + P * t
-                    nc.tensor.transpose(zt[:, t, :], z_tiles[i][:, first : first + P], ident[:])
-                z_banks[i].append(zt)
+        def pair_and_pass(k):
+            pair = [t for t in (2 * (k // 2), 2 * (k // 2) + 1) if t < TILES]
+            return pair, k % 2
 
-        def gain_shift_relu1(i):
-            planes = work.tile([P, PASSES2, PACK, P], BF16)
-            for c in range(PASSES2):
-                for t in range(PACK):
-                    j = PACK * c + t
-                    nc.scalar.activation(
-                        out=planes[:, c, t, :], in_=z_banks[i][c][:, t, :], func=ACT.Relu,
-                        scale=gb[:, j : j + 1], bias=gb[:, D2 // P + j : D2 // P + j + 1],
-                    )
-            j_planes[i] = planes
+        def transpose_z(k):
+            pair, c = pair_and_pass(k)
+            z_banks[k] = []
+            for b in range(2):
+                zt = psum.tile([P, 2, 2, P], F32)
+                for tt in range(2):
+                    first = K_PASS * c + P * (2 * b + tt)
+                    for s, tile_index in enumerate(pair):
+                        nc.tensor.transpose(
+                            zt[:, tt, s, :], z_tiles[tile_index][:, first : first + P], ident[:]
+                        )
+                z_banks[k].append(zt)
 
-        def regroup_j1(i):
-            jg = work.tile([P, PASSES2, P, PACK], BF16, align_bytes=64)
-            nc.vector.tensor_copy(out=jg[:], in_=j_planes[i][:].rearrange("p c t n -> p c n t"))
-            j_grouped[i] = jg
+        def gain_shift_relu1(k):
+            pair, c = pair_and_pass(k)
+            planes = work.tile([P, PACK, 2, P], BF16)
+            for t in range(PACK):
+                j = PACK * c + t
+                nc.scalar.activation(
+                    out=planes[:, t, 0 : len(pair), :], in_=z_banks[k][t // 2][:, t % 2, 0 : len(pair), :],
+                    func=ACT.Relu, scale=gb[:, j : j + 1], bias=gb[:, D2 // P + j : D2 // P + j + 1],
+                )
+            j_planes[k] = planes
 
-        def quantise_j1(i):
-            jc = work.tile([P, PASSES2 * P], U32, align_bytes=64)
-            js = work.tile([P, PASSES2 * P], U8, align_bytes=64)
-            nc.vector.quantize_mx(
-                out=jc[:].bitcast(FP8X4), scales=js[:],
-                in_=j_grouped[i][:].rearrange("p c n t -> p (c n t)"),
+        def regroup_j1(k):
+            pair, c = pair_and_pass(k)
+            jg = work.tile([P, 2 * P, PACK], BF16, align_bytes=64)
+            regroup(
+                nc.vector.tensor_copy,
+                jg[:, 0 : len(pair) * P, :],
+                j_planes[k][:, :, 0 : len(pair), :].rearrange("p t s n -> p t (s n)"),
             )
-            j_codes[i] = jc
-            j_scales[i] = js
+            j_grouped[k] = jg
+
+        def quantise_j1(k):
+            pair, c = pair_and_pass(k)
+            tokens = len(pair) * P
+            jc = work.tile([P, 2 * P], U32, align_bytes=64, bufs=4)
+            js = work.tile([P, 2 * P], U8, align_bytes=64, bufs=4)
+            nc.vector.quantize_mx(
+                out=jc[:, 0:tokens].bitcast(FP8X4), scales=js[:, 0:tokens],
+                in_=j_grouped[k][:, 0:tokens, :].rearrange("p n t -> p (n t)"),
+            )
+            j_codes[k] = jc
+            j_scales[k] = js
 
         def second_product(i):
             acc2 = psum.tile([P, BANK], F32)
+            toks = slice((i % 2) * P, (i % 2 + 1) * P)
             for c in range(PASSES2):
-                toks = slice(c * P, (c + 1) * P)
+                k = PASSES2 * (i // 2) + c
                 nc.tensor.matmul_mx(
                     out=acc2[:],
-                    lhsT=j_codes[i][:, toks].bitcast(FP8X4),
-                    lhsT_scale=j_scales[i][:, toks],
+                    lhsT=j_codes[k][:, toks].bitcast(FP8X4),
+                    lhsT_scale=j_scales[k][:, toks],
                     rhs=w2_codes[:, c, :].bitcast(FP8X4),
                     rhs_scale=w2_scales[:, c, :],
                     start=(c == 0),
@@ -360,30 +377,34 @@ def tile_multiheadedattention_pa_kernel(tc, query, A1W, A1b, g1, b1, A2W, A2b, g
             if 0 <= i < TILES:
                 step(i)
 
+        def run_pair(step, k):
+            if 0 <= k < PASSES2 * PAIRS:
+                step(k)
+
         def period(i):
             if Q_BUFS <= i + Q_BUFS < TILES:
                 load_query(i + Q_BUFS)
-            run(transpose_z, i - 2)
+            run_pair(transpose_z, i - 3)
             run(transpose_query, i + 1)
-            run(regroup_j1, i - 3)
+            run_pair(regroup_j1, i - 4)
             run(quantise_query, i)
             if 0 <= i - 1 < PASSES2:
                 quantise_w2(i - 1)
-            run(quantise_j1, i - 3)
-            run(deviation2, i - 4)
+            run_pair(quantise_j1, i - 4)
+            run(deviation2, i - 6)
             run(deviation1, i - 1)
             run(first_product, i)
-            run(second_product, i - 3)
-            run(centre_gain2, i - 4)
-            run(relu_and_store, i - 5)
-            run(scale_shift2, i - 4)
+            run(second_product, i - 5)
+            run(centre_gain2, i - 6)
+            run(relu_and_store, i - 7)
+            run(scale_shift2, i - 6)
             run(normalise1, i - 1)
             run(query_out_of_psum, i + 1)
-            run(gain_shift_relu1, i - 2)
+            run_pair(gain_shift_relu1, i - 3)
             if 0 <= i < PASSES2:
                 regroup_w2(i)
             run(add_bias1, i)
-            run(add_bias2, i - 3)
+            run(add_bias2, i - 5)
 
         prepare_w1(0)
         prepare_w1(1)
@@ -391,5 +412,5 @@ def tile_multiheadedattention_pa_kernel(tc, query, A1W, A1b, g1, b1, A2W, A2b, g
         prepare_w1(2)
         prepare_w1(3)
         quantise_w1(PASSES1 - 1, 1)
-        for i in range(TILES + 5):
+        for i in range(TILES + 8):
             period(i)

@@ -25,7 +25,6 @@ TILES = TOKENS // P
 PASSES1 = D // K_PASS
 PASSES2 = D2 // K_PASS
 HALVES1 = D2 // BANK
-PAIRS = (TILES + 1) // 2
 
 FLOPS = 2 * TOKENS * (D * D2 + D2 * D4)
 
@@ -195,29 +194,27 @@ def tile_multiheadedattention_pa_kernel(tc, query, A1W, A1b, g1, b1, A2W, A2b, g
             q_grouped[i] = qg
 
         def quantise_query(i):
-            qc = work.tile([P, PASSES1 * P], U32, align_bytes=64)
-            qs = work.tile([P, PASSES1 * P], U8, align_bytes=64)
+            qc = work.tile([P, PASSES1 * P], U32, align_bytes=64, bufs=3)
+            qs = work.tile([P, PASSES1 * P], U8, align_bytes=64, bufs=3)
             nc.vector.quantize_mx(out=qc[:].bitcast(FP8X4), scales=qs[:], in_=q_grouped[i][:])
             q_codes[i] = qc
             q_scales[i] = qs
 
-        def first_product(i):
-            u_banks[i] = []
-            for h in range(HALVES1):
-                cols = slice(h * BANK, (h + 1) * BANK)
-                acc1 = psum.tile([P, BANK], F32)
-                for g in range(PASSES1):
-                    toks = slice(g * P, (g + 1) * P)
-                    nc.tensor.matmul_mx(
-                        out=acc1[:],
-                        lhsT=q_codes[i][:, toks].bitcast(FP8X4),
-                        lhsT_scale=q_scales[i][:, toks],
-                        rhs=w1_codes[:, g, cols].bitcast(FP8X4),
-                        rhs_scale=w1_scales[:, g, cols],
-                        start=(g == 0),
-                        stop=(g == PASSES1 - 1),
-                    )
-                u_banks[i].append(acc1)
+        def first_product(i, h):
+            cols = slice(h * BANK, (h + 1) * BANK)
+            acc1 = psum.tile([P, BANK], F32)
+            for g in range(PASSES1):
+                toks = slice(g * P, (g + 1) * P)
+                nc.tensor.matmul_mx(
+                    out=acc1[:],
+                    lhsT=q_codes[i][:, toks].bitcast(FP8X4),
+                    lhsT_scale=q_scales[i][:, toks],
+                    rhs=w1_codes[:, g, cols].bitcast(FP8X4),
+                    rhs_scale=w1_scales[:, g, cols],
+                    start=(g == 0),
+                    stop=(g == PASSES1 - 1),
+                )
+            u_banks[i, h] = acc1
 
         def add_bias1(i):
             u = work.tile([P, D2], F32)
@@ -225,7 +222,7 @@ def tile_multiheadedattention_pa_kernel(tc, query, A1W, A1b, g1, b1, A2W, A2b, g
             for h in range(HALVES1):
                 cols = slice(h * BANK, (h + 1) * BANK)
                 nc.vector.scalar_tensor_tensor(
-                    out=u[:, cols], in0=u_banks[i][h][:], scalar=1.0, in1=a1_all[:, cols],
+                    out=u[:, cols], in0=u_banks[i, h][:], scalar=1.0, in1=a1_all[:, cols],
                     op0=ALU.mult, op1=ALU.add, accum_out=row_sum[:, h : h + 1],
                 )
             neg_mean = small.tile([P, 1], F32)
@@ -250,72 +247,56 @@ def tile_multiheadedattention_pa_kernel(tc, query, A1W, A1b, g1, b1, A2W, A2b, g
             stats1[i]["rstd"] = rstd
 
         def normalise1(i):
-            z = work.tile([P, D2], F32, bufs=4)
+            z = work.tile([P, D2], F32)
             nc.vector.tensor_scalar(
                 out=z[:], in0=u_tiles[i][:], scalar1=stats1[i]["neg_mean"][:], scalar2=stats1[i]["rstd"][:],
                 op0=ALU.add, op1=ALU.mult,
             )
             z_tiles[i] = z
 
-        def pair_and_pass(k):
-            pair = [t for t in (2 * (k // 2), 2 * (k // 2) + 1) if t < TILES]
-            return pair, k % 2
+        def transpose_z(i):
+            z_banks[i] = []
+            for c in range(PASSES2):
+                zt = psum.tile([P, PACK, P], F32)
+                for t in range(PACK):
+                    first = K_PASS * c + P * t
+                    nc.tensor.transpose(zt[:, t, :], z_tiles[i][:, first : first + P], ident[:])
+                z_banks[i].append(zt)
 
-        def transpose_z(k):
-            pair, c = pair_and_pass(k)
-            z_banks[k] = []
-            for b in range(2):
-                zt = psum.tile([P, 2, 2, P], F32)
-                for tt in range(2):
-                    first = K_PASS * c + P * (2 * b + tt)
-                    for s, tile_index in enumerate(pair):
-                        nc.tensor.transpose(
-                            zt[:, tt, s, :], z_tiles[tile_index][:, first : first + P], ident[:]
-                        )
-                z_banks[k].append(zt)
+        def gain_shift_relu1(i):
+            planes = work.tile([P, PASSES2, PACK, P], BF16)
+            for c in range(PASSES2):
+                for t in range(PACK):
+                    j = PACK * c + t
+                    nc.scalar.activation(
+                        out=planes[:, c, t, :], in_=z_banks[i][c][:, t, :], func=ACT.Relu,
+                        scale=gb[:, j : j + 1], bias=gb[:, D2 // P + j : D2 // P + j + 1],
+                    )
+            j_planes[i] = planes
 
-        def gain_shift_relu1(k):
-            pair, c = pair_and_pass(k)
-            planes = work.tile([P, PACK, 2, P], BF16)
-            for t in range(PACK):
-                j = PACK * c + t
-                nc.scalar.activation(
-                    out=planes[:, t, 0 : len(pair), :], in_=z_banks[k][t // 2][:, t % 2, 0 : len(pair), :],
-                    func=ACT.Relu, scale=gb[:, j : j + 1], bias=gb[:, D2 // P + j : D2 // P + j + 1],
-                )
-            j_planes[k] = planes
+        def regroup_j1(i):
+            jg = work.tile([P, PASSES2, P, PACK], BF16, align_bytes=64)
+            nc.vector.tensor_copy(out=jg[:], in_=j_planes[i][:].rearrange("p c t n -> p c n t"))
+            j_grouped[i] = jg
 
-        def regroup_j1(k):
-            pair, c = pair_and_pass(k)
-            jg = work.tile([P, 2 * P, PACK], BF16, align_bytes=64)
-            regroup(
-                nc.vector.tensor_copy,
-                jg[:, 0 : len(pair) * P, :],
-                j_planes[k][:, :, 0 : len(pair), :].rearrange("p t s n -> p t (s n)"),
-            )
-            j_grouped[k] = jg
-
-        def quantise_j1(k):
-            pair, c = pair_and_pass(k)
-            tokens = len(pair) * P
-            jc = work.tile([P, 2 * P], U32, align_bytes=64, bufs=4)
-            js = work.tile([P, 2 * P], U8, align_bytes=64, bufs=4)
+        def quantise_j1(i):
+            jc = work.tile([P, PASSES2 * P], U32, align_bytes=64)
+            js = work.tile([P, PASSES2 * P], U8, align_bytes=64)
             nc.vector.quantize_mx(
-                out=jc[:, 0:tokens].bitcast(FP8X4), scales=js[:, 0:tokens],
-                in_=j_grouped[k][:, 0:tokens, :].rearrange("p n t -> p (n t)"),
+                out=jc[:].bitcast(FP8X4), scales=js[:],
+                in_=j_grouped[i][:].rearrange("p c n t -> p (c n t)"),
             )
-            j_codes[k] = jc
-            j_scales[k] = js
+            j_codes[i] = jc
+            j_scales[i] = js
 
         def second_product(i):
             acc2 = psum.tile([P, BANK], F32)
-            toks = slice((i % 2) * P, (i % 2 + 1) * P)
             for c in range(PASSES2):
-                k = PASSES2 * (i // 2) + c
+                toks = slice(c * P, (c + 1) * P)
                 nc.tensor.matmul_mx(
                     out=acc2[:],
-                    lhsT=j_codes[k][:, toks].bitcast(FP8X4),
-                    lhsT_scale=j_scales[k][:, toks],
+                    lhsT=j_codes[i][:, toks].bitcast(FP8X4),
+                    lhsT_scale=j_scales[i][:, toks],
                     rhs=w2_codes[:, c, :].bitcast(FP8X4),
                     rhs_scale=w2_scales[:, c, :],
                     start=(c == 0),
@@ -373,44 +354,41 @@ def tile_multiheadedattention_pa_kernel(tc, query, A1W, A1b, g1, b1, A2W, A2b, g
             nc.vector.tensor_scalar_max(out=result[:], in0=y_tiles[i][:], scalar1=0.0)
             nc.sync.dma_start(out=out_rows[i * P : (i + 1) * P, :], in_=result[:])
 
-        def run(step, i):
+        def run(step, i, *more):
             if 0 <= i < TILES:
-                step(i)
-
-        def run_pair(step, k):
-            if 0 <= k < PASSES2 * PAIRS:
-                step(k)
+                step(i, *more)
 
         def period(i):
-            if Q_BUFS <= i + Q_BUFS < TILES:
-                load_query(i + Q_BUFS)
-            run_pair(transpose_z, i - 3)
-            run(transpose_query, i + 1)
-            run_pair(regroup_j1, i - 4)
-            run(quantise_query, i)
+            if Q_BUFS <= i + 1 + Q_BUFS < TILES:
+                load_query(i + 1 + Q_BUFS)
+            run(first_product, i, 0)
+            run(transpose_z, i - 2)
+            run(first_product, i, 1)
+            run(transpose_query, i + 2)
+            run(regroup_j1, i - 3)
+            run(quantise_query, i + 1)
             if 0 <= i - 1 < PASSES2:
                 quantise_w2(i - 1)
-            run_pair(quantise_j1, i - 4)
-            run(deviation2, i - 6)
+            run(quantise_j1, i - 3)
+            run(second_product, i - 3)
+            run(deviation2, i - 4)
             run(deviation1, i - 1)
-            run(first_product, i)
-            run(second_product, i - 5)
-            run(centre_gain2, i - 6)
-            run(relu_and_store, i - 7)
-            run(scale_shift2, i - 6)
+            run(centre_gain2, i - 4)
+            run(relu_and_store, i - 5)
+            run(scale_shift2, i - 4)
             run(normalise1, i - 1)
-            run(query_out_of_psum, i + 1)
-            run_pair(gain_shift_relu1, i - 3)
+            run(gain_shift_relu1, i - 2)
+            run(query_out_of_psum, i + 2)
             if 0 <= i < PASSES2:
                 regroup_w2(i)
             run(add_bias1, i)
-            run(add_bias2, i - 5)
+            run(add_bias2, i - 3)
 
         prepare_w1(0)
         prepare_w1(1)
-        period(-1)
+        period(-2)
         prepare_w1(2)
         prepare_w1(3)
         quantise_w1(PASSES1 - 1, 1)
-        for i in range(TILES + 8):
+        for i in range(-1, TILES + 5):
             period(i)

@@ -29,6 +29,8 @@ HALVES1 = D2 // BANK
 FLOPS = 2 * TOKENS * (D * D2 + D2 * D4)
 
 Q_BUFS = 8
+W2_REGROUP_PERIOD = -1
+W2_QUANTISE_PERIOD = 1
 
 
 def tile_multiheadedattention_pa_kernel(tc, query, A1W, A1b, g1, b1, A2W, A2b, g2, b2, out):
@@ -82,20 +84,19 @@ def tile_multiheadedattention_pa_kernel(tc, query, A1W, A1b, g1, b1, A2W, A2b, g
             nc.sync.dma_start(out=spread[:], in_=vec.partition_broadcast(P))
             return spread
 
-        load_w1(0)
-        load_w1(1)
         load_query(0)
-        load_w1(2)
-        load_w1(3)
+        for g in range(PASSES1):
+            load_w1(g)
         a1_all = load_row_to_all_partitions(A1b, D2, "a1_all")
         load_query(1)
+        for c in range(PASSES2):
+            load_w2(c)
         load_query(2)
-        load_w2(0)
-        load_w2(1)
+        load_query(3)
         a2_all = load_row_to_all_partitions(A2b, D4, "a2_all")
         g2_all = load_row_to_all_partitions(g2, D4, "g2_all")
         b2_all = load_row_to_all_partitions(b2, D4, "b2_all")
-        for i in range(3, Q_BUFS):
+        for i in range(4, Q_BUFS):
             load_query(i)
 
         gb_square = keep.tile([P, P], F32)
@@ -225,13 +226,17 @@ def tile_multiheadedattention_pa_kernel(tc, query, A1W, A1b, g1, b1, A2W, A2b, g
                     out=u[:, cols], in0=u_banks[i, h][:], scalar=1.0, in1=a1_all[:, cols],
                     op0=ALU.mult, op1=ALU.add, accum_out=row_sum[:, h : h + 1],
                 )
+            u_tiles[i] = u
+            stats1[i] = {"row_sum": row_sum}
+
+        def mean1(i):
+            row_sum = stats1[i]["row_sum"]
             neg_mean = small.tile([P, 1], F32)
             nc.vector.tensor_scalar(
                 out=neg_mean[:], in0=row_sum[:, 0:1], scalar1=row_sum[:, 1:2], scalar2=-1.0 / D2,
                 op0=ALU.add, op1=ALU.mult,
             )
-            u_tiles[i] = u
-            stats1[i] = {"neg_mean": neg_mean}
+            stats1[i]["neg_mean"] = neg_mean
 
         def deviation1(i):
             squares = work.tile([P, D2], F32)
@@ -240,9 +245,13 @@ def tile_multiheadedattention_pa_kernel(tc, query, A1W, A1b, g1, b1, A2W, A2b, g
                 out=squares[:], in_=u_tiles[i][:], func=ACT.Square,
                 bias=stats1[i]["neg_mean"][:], scale=1.0, accum_out=sq_sum[:],
             )
+            stats1[i]["sq_sum"] = sq_sum
+
+        def inverse_deviation1(i):
             rstd = small.tile([P, 1], F32)
             nc.scalar.activation(
-                out=rstd[:], in_=sq_sum[:], func=ACT.Abs_reciprocal_sqrt, bias=eps[:], scale=1.0 / D2,
+                out=rstd[:], in_=stats1[i]["sq_sum"][:], func=ACT.Abs_reciprocal_sqrt,
+                bias=eps[:], scale=1.0 / D2,
             )
             stats1[i]["rstd"] = rstd
 
@@ -264,19 +273,19 @@ def tile_multiheadedattention_pa_kernel(tc, query, A1W, A1b, g1, b1, A2W, A2b, g
                 z_banks[i].append(zt)
 
         def gain_shift_relu1(i):
-            planes = work.tile([P, PASSES2, PACK, P], BF16)
+            planes = work.tile([P, PACK, PASSES2, P], BF16)
             for c in range(PASSES2):
                 for t in range(PACK):
                     j = PACK * c + t
                     nc.scalar.activation(
-                        out=planes[:, c, t, :], in_=z_banks[i][c][:, t, :], func=ACT.Relu,
+                        out=planes[:, t, c, :], in_=z_banks[i][c][:, t, :], func=ACT.Relu,
                         scale=gb[:, j : j + 1], bias=gb[:, D2 // P + j : D2 // P + j + 1],
                     )
             j_planes[i] = planes
 
         def regroup_j1(i):
-            jg = work.tile([P, PASSES2, P, PACK], BF16, align_bytes=64)
-            nc.vector.tensor_copy(out=jg[:], in_=j_planes[i][:].rearrange("p c t n -> p c n t"))
+            jg = work.tile([P, PASSES2 * P, PACK], BF16, align_bytes=64)
+            regroup(nc.vector.tensor_copy, jg[:], j_planes[i][:].rearrange("p t c n -> p t (c n)"))
             j_grouped[i] = jg
 
         def quantise_j1(i):
@@ -284,7 +293,7 @@ def tile_multiheadedattention_pa_kernel(tc, query, A1W, A1b, g1, b1, A2W, A2b, g
             js = work.tile([P, PASSES2 * P], U8, align_bytes=64)
             nc.vector.quantize_mx(
                 out=jc[:].bitcast(FP8X4), scales=js[:],
-                in_=j_grouped[i][:].rearrange("p c n t -> p (c n t)"),
+                in_=j_grouped[i][:].rearrange("p n t -> p (n t)"),
             )
             j_codes[i] = jc
             j_scales[i] = js
@@ -311,12 +320,16 @@ def tile_multiheadedattention_pa_kernel(tc, query, A1W, A1b, g1, b1, A2W, A2b, g
                 out=w[:], in0=w_banks[i][:], scalar=1.0, in1=a2_all[:],
                 op0=ALU.mult, op1=ALU.add, accum_out=row_sum2[:],
             )
+            w_tiles[i] = w
+            stats2[i] = {"row_sum": row_sum2}
+
+        def mean2(i):
             neg_mean2 = small.tile([P, 1], F32)
             nc.vector.tensor_scalar(
-                out=neg_mean2[:], in0=row_sum2[:], scalar1=-1.0 / D4, scalar2=None, op0=ALU.mult,
+                out=neg_mean2[:], in0=stats2[i]["row_sum"][:], scalar1=-1.0 / D4, scalar2=None,
+                op0=ALU.mult,
             )
-            w_tiles[i] = w
-            stats2[i] = {"neg_mean": neg_mean2}
+            stats2[i]["neg_mean"] = neg_mean2
 
         def deviation2(i):
             squares2 = work.tile([P, D4], F32)
@@ -325,9 +338,13 @@ def tile_multiheadedattention_pa_kernel(tc, query, A1W, A1b, g1, b1, A2W, A2b, g
                 out=squares2[:], in_=w_tiles[i][:], func=ACT.Square,
                 bias=stats2[i]["neg_mean"][:], scale=1.0, accum_out=sq_sum2[:],
             )
+            stats2[i]["sq_sum"] = sq_sum2
+
+        def inverse_deviation2(i):
             rstd2 = small.tile([P, 1], F32)
             nc.scalar.activation(
-                out=rstd2[:], in_=sq_sum2[:], func=ACT.Abs_reciprocal_sqrt, bias=eps[:], scale=1.0 / D4,
+                out=rstd2[:], in_=stats2[i]["sq_sum"][:], func=ACT.Abs_reciprocal_sqrt,
+                bias=eps[:], scale=1.0 / D4,
             )
             stats2[i]["rstd"] = rstd2
 
@@ -366,29 +383,33 @@ def tile_multiheadedattention_pa_kernel(tc, query, A1W, A1b, g1, b1, A2W, A2b, g
             run(first_product, i, 1)
             run(transpose_query, i + 2)
             run(regroup_j1, i - 3)
+            run(mean2, i - 4)
             run(quantise_query, i + 1)
-            if 0 <= i - 1 < PASSES2:
-                quantise_w2(i - 1)
+            if i == W2_QUANTISE_PERIOD:
+                for c in range(PASSES2):
+                    quantise_w2(c)
             run(quantise_j1, i - 3)
             run(second_product, i - 3)
-            run(deviation2, i - 4)
             run(deviation1, i - 1)
+            run(deviation2, i - 4)
+            run(inverse_deviation1, i - 1)
+            run(inverse_deviation2, i - 4)
             run(centre_gain2, i - 4)
             run(relu_and_store, i - 5)
-            run(scale_shift2, i - 4)
             run(normalise1, i - 1)
+            run(scale_shift2, i - 4)
             run(gain_shift_relu1, i - 2)
             run(query_out_of_psum, i + 2)
-            if 0 <= i < PASSES2:
-                regroup_w2(i)
+            if i == W2_REGROUP_PERIOD:
+                for c in range(PASSES2):
+                    regroup_w2(c)
             run(add_bias1, i)
             run(add_bias2, i - 3)
+            run(mean1, i)
 
-        prepare_w1(0)
-        prepare_w1(1)
         period(-2)
-        prepare_w1(2)
-        prepare_w1(3)
+        for g in range(PASSES1):
+            prepare_w1(g)
         quantise_w1(PASSES1 - 1, 1)
         for i in range(-1, TILES + 5):
             period(i)

@@ -29,6 +29,7 @@ HALVES1 = D2 // BANK
 FLOPS = 2 * TOKENS * (D * D2 + D2 * D4)
 
 Q_BUFS = 8
+W1_PERIOD = -1
 W2_REGROUP_PERIOD = -1
 W2_QUANTISE_PERIOD = 1
 
@@ -368,7 +369,7 @@ def tile_multiheadedattention_pa_kernel(tc, query, A1W, A1b, g1, b1, A2W, A2b, g
 
         def relu_and_store(i):
             result = work.tile([P, D4], F32, bufs=3)
-            nc.vector.tensor_scalar_max(out=result[:], in0=y_tiles[i][:], scalar1=0.0)
+            nc.scalar.activation(out=result[:], in_=y_tiles[i][:], func=ACT.Relu)
             nc.sync.dma_start(out=out_rows[i * P : (i + 1) * P, :], in_=result[:])
 
         def run(step, i, *more):
@@ -379,37 +380,37 @@ def tile_multiheadedattention_pa_kernel(tc, query, A1W, A1b, g1, b1, A2W, A2b, g
             if Q_BUFS <= i + 1 + Q_BUFS < TILES:
                 load_query(i + 1 + Q_BUFS)
             run(first_product, i, 0)
-            run(transpose_z, i - 2)
-            run(first_product, i, 1)
             run(transpose_query, i + 2)
+            run(first_product, i, 1)
+            run(transpose_z, i - 2)
             run(regroup_j1, i - 3)
             run(mean2, i - 4)
             run(quantise_query, i + 1)
-            if i == W2_QUANTISE_PERIOD:
-                for c in range(PASSES2):
-                    quantise_w2(c)
+            if i == W1_PERIOD:
+                for g in range(PASSES1):
+                    prepare_w1(g)
+                quantise_w1(PASSES1 - 1, 1)
             run(quantise_j1, i - 3)
+            run(centre_gain2, i - 4)
             run(second_product, i - 3)
             run(deviation1, i - 1)
             run(deviation2, i - 4)
-            run(inverse_deviation1, i - 1)
-            run(inverse_deviation2, i - 4)
-            run(centre_gain2, i - 4)
-            run(relu_and_store, i - 5)
-            run(normalise1, i - 1)
-            run(scale_shift2, i - 4)
-            run(gain_shift_relu1, i - 2)
             run(query_out_of_psum, i + 2)
             if i == W2_REGROUP_PERIOD:
                 for c in range(PASSES2):
                     regroup_w2(c)
+            run(inverse_deviation1, i - 1)
+            run(inverse_deviation2, i - 4)
+            run(gain_shift_relu1, i - 2)
+            run(relu_and_store, i - 5)
             run(add_bias1, i)
-            run(add_bias2, i - 3)
+            run(normalise1, i - 1)
+            run(scale_shift2, i - 4)
             run(mean1, i)
+            run(add_bias2, i - 3)
+            if i == W2_QUANTISE_PERIOD:
+                for c in range(PASSES2):
+                    quantise_w2(c)
 
-        period(-2)
-        for g in range(PASSES1):
-            prepare_w1(g)
-        quantise_w1(PASSES1 - 1, 1)
-        for i in range(-1, TILES + 5):
+        for i in range(-2, TILES + 5):
             period(i)

@@ -61,6 +61,14 @@ def tile_multiheadedattention_pa_kernel(tc, query, A1W, A1b, g1, b1, A2W, A2b, g
         nc.sync.dma_start(out=gb_rows[0 : D2 // P, :], in_=g1.rearrange("(j p) -> j p", p=P))
         nc.sync.dma_start(out=gb_rows[D2 // P : 2 * D2 // P, :], in_=b1.rearrange("(j p) -> j p", p=P))
 
+        vectors = ((A1b, D2), (A2b, D4), (g2, D4), (b2, D4))
+        row0 = keep.tile([P, D2 + 3 * D4], BF16)
+        nc.vector.memset(row0[:], 0.0)
+        start = 0
+        for vec, width in vectors:
+            nc.sync.dma_start(out=row0[0:1, start : start + width], in_=vec.rearrange("(o n) -> o n", o=1))
+            start += width
+
         q_tiles = {}
         w1_raw = {}
         w2_raw = {}
@@ -80,23 +88,14 @@ def tile_multiheadedattention_pa_kernel(tc, query, A1W, A1b, g1, b1, A2W, A2b, g
             nc.sync.dma_start(out=raw2[:], in_=w2_view[c])
             w2_raw[c] = raw2
 
-        def load_row_to_all_partitions(vec, width, name):
-            spread = keep.tile([P, width], BF16, name=name)
-            nc.sync.dma_start(out=spread[:], in_=vec.partition_broadcast(P))
-            return spread
-
         load_query(0)
         for g in range(PASSES1):
             load_w1(g)
-        a1_all = load_row_to_all_partitions(A1b, D2, "a1_all")
         load_query(1)
         for c in range(PASSES2):
             load_w2(c)
         load_query(2)
         load_query(3)
-        a2_all = load_row_to_all_partitions(A2b, D4, "a2_all")
-        g2_all = load_row_to_all_partitions(g2, D4, "g2_all")
-        b2_all = load_row_to_all_partitions(b2, D4, "b2_all")
         for i in range(4, Q_BUFS):
             load_query(i)
 
@@ -107,6 +106,22 @@ def tile_multiheadedattention_pa_kernel(tc, query, A1W, A1b, g1, b1, A2W, A2b, g
         nc.tensor.transpose(gb_t[:], gb_square[:], ident[:])
         gb = keep.tile([P, 2 * D2 // P], F32)
         nc.vector.tensor_copy(out=gb[:], in_=gb_t[:, 0 : 2 * D2 // P])
+
+        ones = keep.tile([P, P], BF16)
+        nc.vector.memset(ones[:], 1.0)
+        on_all = keep.tile([P, D2 + 3 * D4], BF16)
+        for j in range((D2 + 3 * D4) // BANK):
+            cols = slice(j * BANK, (j + 1) * BANK)
+            spread = psum.tile([P, BANK], F32, tag="acc1")
+            nc.tensor.matmul(out=spread[:], lhsT=ones[:], rhs=row0[:, cols], start=True, stop=True)
+            if j % 2 == 0:
+                nc.scalar.copy(out=on_all[:, cols], in_=spread[:])
+            else:
+                nc.vector.tensor_copy(out=on_all[:, cols], in_=spread[:])
+        a1_all = on_all[:, 0:D2]
+        a2_all = on_all[:, D2 : D2 + D4]
+        g2_all = on_all[:, D2 + D4 : D2 + 2 * D4]
+        b2_all = on_all[:, D2 + 2 * D4 : D2 + 3 * D4]
 
         w1_codes = keep.tile([P, PASSES1, D2], U32, align_bytes=64)
         w1_scales = keep.tile([P, PASSES1, D2], U8, align_bytes=64)
@@ -318,7 +333,7 @@ def tile_multiheadedattention_pa_kernel(tc, query, A1W, A1b, g1, b1, A2W, A2b, g
             w = work.tile([P, D4], F32, bufs=3)
             row_sum2 = small.tile([P, 1], F32)
             nc.vector.scalar_tensor_tensor(
-                out=w[:], in0=w_banks[i][:], scalar=1.0, in1=a2_all[:],
+                out=w[:], in0=w_banks[i][:], scalar=1.0, in1=a2_all,
                 op0=ALU.mult, op1=ALU.add, accum_out=row_sum2[:],
             )
             w_tiles[i] = w
@@ -354,7 +369,7 @@ def tile_multiheadedattention_pa_kernel(tc, query, A1W, A1b, g1, b1, A2W, A2b, g
         def centre_gain2(i):
             x = work.tile([P, D4], F32)
             nc.vector.scalar_tensor_tensor(
-                out=x[:], in0=w_tiles[i][:], scalar=stats2[i]["neg_mean"][:], in1=g2_all[:],
+                out=x[:], in0=w_tiles[i][:], scalar=stats2[i]["neg_mean"][:], in1=g2_all,
                 op0=ALU.add, op1=ALU.mult,
             )
             x_tiles[i] = x
@@ -362,7 +377,7 @@ def tile_multiheadedattention_pa_kernel(tc, query, A1W, A1b, g1, b1, A2W, A2b, g
         def scale_shift2(i):
             y = work.tile([P, D4], F32)
             nc.vector.scalar_tensor_tensor(
-                out=y[:], in0=x_tiles[i][:], scalar=stats2[i]["rstd"][:], in1=b2_all[:],
+                out=y[:], in0=x_tiles[i][:], scalar=stats2[i]["rstd"][:], in1=b2_all,
                 op0=ALU.mult, op1=ALU.add,
             )
             y_tiles[i] = y

@@ -48,7 +48,6 @@ def tile_multiheadedattention_pa_kernel(tc, query, A1W, A1b, g1, b1, A2W, A2b, g
         work = ctx.enter_context(tc.tile_pool(name="work", bufs=2))
         small = ctx.enter_context(tc.tile_pool(name="small", bufs=4))
         psum = ctx.enter_context(tc.psum_pool(name="psum", bufs=2))
-        ctx.enter_context(tc.manual_schedule())
 
         ident = keep.tile([P, P], F32)
         make_identity(nc, ident[:])
@@ -60,14 +59,6 @@ def tile_multiheadedattention_pa_kernel(tc, query, A1W, A1b, g1, b1, A2W, A2b, g
         gb_rows = keep.tile([2 * D2 // P, P], BF16)
         nc.sync.dma_start(out=gb_rows[0 : D2 // P, :], in_=g1.rearrange("(j p) -> j p", p=P))
         nc.sync.dma_start(out=gb_rows[D2 // P : 2 * D2 // P, :], in_=b1.rearrange("(j p) -> j p", p=P))
-
-        vectors = ((A1b, D2), (A2b, D4), (g2, D4), (b2, D4))
-        row0 = keep.tile([P, D2 + 3 * D4], BF16)
-        nc.vector.memset(row0[:], 0.0)
-        start = 0
-        for vec, width in vectors:
-            nc.sync.dma_start(out=row0[0:1, start : start + width], in_=vec.rearrange("(o n) -> o n", o=1))
-            start += width
 
         q_tiles = {}
         w1_raw = {}
@@ -88,14 +79,23 @@ def tile_multiheadedattention_pa_kernel(tc, query, A1W, A1b, g1, b1, A2W, A2b, g
             nc.sync.dma_start(out=raw2[:], in_=w2_view[c])
             w2_raw[c] = raw2
 
+        def load_row_to_all_partitions(vec, width, name):
+            spread = keep.tile([P, width], BF16, name=name)
+            nc.sync.dma_start(out=spread[:], in_=vec.partition_broadcast(P))
+            return spread
+
         load_query(0)
         for g in range(PASSES1):
             load_w1(g)
+        a1_all = load_row_to_all_partitions(A1b, D2, "a1_all")
         load_query(1)
         for c in range(PASSES2):
             load_w2(c)
         load_query(2)
         load_query(3)
+        a2_all = load_row_to_all_partitions(A2b, D4, "a2_all")
+        g2_all = load_row_to_all_partitions(g2, D4, "g2_all")
+        b2_all = load_row_to_all_partitions(b2, D4, "b2_all")
         for i in range(4, Q_BUFS):
             load_query(i)
 
@@ -106,22 +106,6 @@ def tile_multiheadedattention_pa_kernel(tc, query, A1W, A1b, g1, b1, A2W, A2b, g
         nc.tensor.transpose(gb_t[:], gb_square[:], ident[:])
         gb = keep.tile([P, 2 * D2 // P], F32)
         nc.vector.tensor_copy(out=gb[:], in_=gb_t[:, 0 : 2 * D2 // P])
-
-        ones = keep.tile([P, P], BF16)
-        nc.vector.memset(ones[:], 1.0)
-        on_all = keep.tile([P, D2 + 3 * D4], BF16)
-        for j in range((D2 + 3 * D4) // BANK):
-            cols = slice(j * BANK, (j + 1) * BANK)
-            spread = psum.tile([P, BANK], F32, tag="acc1")
-            nc.tensor.matmul(out=spread[:], lhsT=ones[:], rhs=row0[:, cols], start=True, stop=True)
-            if j % 2 == 0:
-                nc.scalar.copy(out=on_all[:, cols], in_=spread[:])
-            else:
-                nc.vector.tensor_copy(out=on_all[:, cols], in_=spread[:])
-        a1_all = on_all[:, 0:D2]
-        a2_all = on_all[:, D2 : D2 + D4]
-        g2_all = on_all[:, D2 + D4 : D2 + 2 * D4]
-        b2_all = on_all[:, D2 + 2 * D4 : D2 + 3 * D4]
 
         w1_codes = keep.tile([P, PASSES1, D2], U32, align_bytes=64)
         w1_scales = keep.tile([P, PASSES1, D2], U8, align_bytes=64)
@@ -333,7 +317,7 @@ def tile_multiheadedattention_pa_kernel(tc, query, A1W, A1b, g1, b1, A2W, A2b, g
             w = work.tile([P, D4], F32, bufs=3)
             row_sum2 = small.tile([P, 1], F32)
             nc.vector.scalar_tensor_tensor(
-                out=w[:], in0=w_banks[i][:], scalar=1.0, in1=a2_all,
+                out=w[:], in0=w_banks[i][:], scalar=1.0, in1=a2_all[:],
                 op0=ALU.mult, op1=ALU.add, accum_out=row_sum2[:],
             )
             w_tiles[i] = w
@@ -369,7 +353,7 @@ def tile_multiheadedattention_pa_kernel(tc, query, A1W, A1b, g1, b1, A2W, A2b, g
         def centre_gain2(i):
             x = work.tile([P, D4], F32)
             nc.vector.scalar_tensor_tensor(
-                out=x[:], in0=w_tiles[i][:], scalar=stats2[i]["neg_mean"][:], in1=g2_all,
+                out=x[:], in0=w_tiles[i][:], scalar=stats2[i]["neg_mean"][:], in1=g2_all[:],
                 op0=ALU.add, op1=ALU.mult,
             )
             x_tiles[i] = x
@@ -377,7 +361,7 @@ def tile_multiheadedattention_pa_kernel(tc, query, A1W, A1b, g1, b1, A2W, A2b, g
         def scale_shift2(i):
             y = work.tile([P, D4], F32)
             nc.vector.scalar_tensor_tensor(
-                out=y[:], in0=x_tiles[i][:], scalar=stats2[i]["rstd"][:], in1=b2_all,
+                out=y[:], in0=x_tiles[i][:], scalar=stats2[i]["rstd"][:], in1=b2_all[:],
                 op0=ALU.mult, op1=ALU.add,
             )
             y_tiles[i] = y

from contextlib import ExitStack

import concourse.mybir as mybir
from concourse.masks import make_identity

F32 = mybir.dt.float32
BF16 = mybir.dt.bfloat16
U32 = mybir.dt.uint32
U8 = mybir.dt.uint8
FP8X4 = mybir.dt.float8_e4m3fn_x4
ALU = mybir.AluOpType
ACT = mybir.ActivationFunctionType

P = 128
PACK = 4
K_PASS = P * PACK
BANK = 512

TOKENS = 128 * 17
D = 2048
D2 = 1024
D4 = 512
EPS = 1e-5
TILES = TOKENS // P
PASSES1 = D // K_PASS
PASSES2 = D2 // K_PASS
HALVES1 = D2 // BANK

FLOPS = 2 * TOKENS * (D * D2 + D2 * D4)

Q_BUFS = 8
W1_PERIOD = -1
W2_REGROUP_PERIOD = -1
W2_QUANTISE_PERIOD = 1


def tile_multiheadedattention_pa_kernel(tc, query, A1W, A1b, g1, b1, A2W, A2b, g2, b2, out):
    nc = tc.nc
    q_rows = query.flatten_outer_dims()
    out_rows = out.flatten_outer_dims()
    w1_view = A1W.rearrange("(g u p e) n -> g p u (e n)", g=PASSES1, u=2, p=P, e=2)
    w2_view = A2W.rearrange("(c t p) n -> c p t n", c=PASSES2, t=PACK, p=P)

    with ExitStack() as ctx:
        keep = ctx.enter_context(tc.tile_pool(name="keep", bufs=1))
        q_pool = ctx.enter_context(tc.tile_pool(name="q_pool", bufs=Q_BUFS))
        w_pool = ctx.enter_context(tc.tile_pool(name="w_pool", bufs=2))
        work = ctx.enter_context(tc.tile_pool(name="work", bufs=2))
        small = ctx.enter_context(tc.tile_pool(name="small", bufs=4))
        psum = ctx.enter_context(tc.psum_pool(name="psum", bufs=2))

        ident = keep.tile([P, P], F32)
        make_identity(nc, ident[:])
        eps = keep.tile([P, 1], F32)
        nc.vector.memset(eps[:], EPS)
        table_warm = keep.tile([P, 1], F32)
        nc.scalar.activation(out=table_warm[:], in_=eps[:], func=ACT.Abs_reciprocal_sqrt)

        gb_rows = keep.tile([2 * D2 // P, P], BF16)
        nc.sync.dma_start(out=gb_rows[0 : D2 // P, :], in_=g1.rearrange("(j p) -> j p", p=P))
        nc.sync.dma_start(out=gb_rows[D2 // P : 2 * D2 // P, :], in_=b1.rearrange("(j p) -> j p", p=P))

        q_tiles = {}
        w1_raw = {}
        w2_raw = {}

        def load_query(i):
            q_sb = q_pool.tile([P, D], BF16)
            nc.sync.dma_start(out=q_sb[:], in_=q_rows[i * P : (i + 1) * P, :])
            q_tiles[i] = q_sb

        def load_w1(g):
            raw1 = keep.tile([P, 2, 2 * D2], BF16, name="raw1_%d" % g)
            nc.sync.dma_start(out=raw1[:], in_=w1_view[g])
            w1_raw[g] = raw1

        def load_w2(c):
            raw2 = keep.tile([P, PACK, D4], BF16, name="raw2_%d" % c)
            nc.sync.dma_start(out=raw2[:], in_=w2_view[c])
            w2_raw[c] = raw2

        def load_row_to_all_partitions(vec, width, name):
            spread = keep.tile([P, width], BF16, name=name)
            nc.sync.dma_start(out=spread[:], in_=vec.partition_broadcast(P))
            return spread

        load_query(0)
        for g in range(PASSES1):
            load_w1(g)
        a1_all = load_row_to_all_partitions(A1b, D2, "a1_all")
        load_query(1)
        for c in range(PASSES2):
            load_w2(c)
        load_query(2)
        load_query(3)
        a2_all = load_row_to_all_partitions(A2b, D4, "a2_all")
        g2_all = load_row_to_all_partitions(g2, D4, "g2_all")
        b2_all = load_row_to_all_partitions(b2, D4, "b2_all")
        for i in range(4, Q_BUFS):
            load_query(i)

        gb_square = keep.tile([P, P], F32)
        nc.vector.memset(gb_square[:], 0.0)
        nc.vector.tensor_copy(out=gb_square[0 : 2 * D2 // P, :], in_=gb_rows[:])
        gb_t = psum.tile([P, P], F32, tag="acc2")
        nc.tensor.transpose(gb_t[:], gb_square[:], ident[:])
        gb = keep.tile([P, 2 * D2 // P], F32)
        nc.vector.tensor_copy(out=gb[:], in_=gb_t[:, 0 : 2 * D2 // P])

        w1_codes = keep.tile([P, PASSES1, D2], U32, align_bytes=64)
        w1_scales = keep.tile([P, PASSES1, D2], U8, align_bytes=64)
        w2_codes = keep.tile([P, PASSES2, D4], U32, align_bytes=64)
        w2_scales = keep.tile([P, PASSES2, D4], U8, align_bytes=64)
        w2_grouped = {}

        def regroup(copy, dst, src):
            copy(
                out=dst.rearrange("p (c i) t -> p c t i", i=4),
                in_=src.rearrange("p t (c i) -> p c t i", i=4),
            )

        w1_grouped = {}

        def regroup_w1(g):
            rows = w1_raw[g][:].rearrange("p u (e n) -> p (u e) n", e=2)
            by_scalar = w_pool.tile([P, BANK, PACK], BF16, align_bytes=64)
            regroup(nc.scalar.copy, by_scalar[:], rows[:, :, BANK : 2 * BANK])
            by_vector = w_pool.tile([P, BANK, PACK], BF16, align_bytes=64)
            regroup(nc.vector.tensor_copy, by_vector[:], rows[:, :, 0:BANK])
            w1_grouped[g] = (by_vector, by_scalar)

        def quantise_w1(g, h):
            cols = slice(h * BANK, (h + 1) * BANK)
            nc.vector.quantize_mx(
                out=w1_codes[:, g, cols].bitcast(FP8X4),
                scales=w1_scales[:, g, cols],
                in_=w1_grouped[g][h][:].rearrange("p n t -> p (n t)"),
            )

        def prepare_w1(g):
            regroup_w1(g)
            if g > 0:
                quantise_w1(g - 1, 1)
            quantise_w1(g, 0)

        def regroup_w2(c):
            grouped2 = keep.tile([P, D4, PACK], BF16, align_bytes=64, name="grouped2_%d" % c)
            regroup(nc.scalar.copy, grouped2[:], w2_raw[c][:])
            w2_grouped[c] = grouped2

        def quantise_w2(c):
            nc.vector.quantize_mx(
                out=w2_codes[:, c, :].bitcast(FP8X4),
                scales=w2_scales[:, c, :],
                in_=w2_grouped[c][:].rearrange("p n t -> p (n t)"),
            )

        q_banks = {}
        q_grouped = {}
        q_codes = {}
        q_scales = {}
        u_banks = {}
        u_tiles = {}
        stats1 = {}
        z_tiles = {}
        z_banks = {}
        j_planes = {}
        j_grouped = {}
        j_codes = {}
        j_scales = {}
        w_banks = {}
        w_tiles = {}
        stats2 = {}
        y_tiles = {}

        def transpose_query(i):
            words = q_tiles[i][:].bitcast(F32)
            q_banks[i] = []
            for b in range(2):
                qt = psum.tile([P, 2, 2, P], F32)
                for gg in range(2):
                    for u in range(2):
                        first = 256 * (2 * b + gg) + P * u
                        nc.tensor.transpose(qt[:, gg, u, :], words[:, first : first + P], ident[:])
                q_banks[i].append(qt)

        def query_out_of_psum(i):
            qg = work.tile([P, PASSES1 * P * PACK], BF16, align_bytes=64)
            qg_words = qg[:].bitcast(F32).rearrange("p (g n u) -> p g n u", g=PASSES1, u=2)
            for b in range(2):
                nc.scalar.copy(
                    out=qg_words[:, 2 * b : 2 * b + 2, :, :],
                    in_=q_banks[i][b][:].rearrange("p g u n -> p g n u"),
                )
            q_grouped[i] = qg

        def quantise_query(i):
            qc = work.tile([P, PASSES1 * P], U32, align_bytes=64, bufs=3)
            qs = work.tile([P, PASSES1 * P], U8, align_bytes=64, bufs=3)
            nc.vector.quantize_mx(out=qc[:].bitcast(FP8X4), scales=qs[:], in_=q_grouped[i][:])
            q_codes[i] = qc
            q_scales[i] = qs

        def first_product(i, h):
            cols = slice(h * BANK, (h + 1) * BANK)
            acc1 = psum.tile([P, BANK], F32)
            for g in range(PASSES1):
                toks = slice(g * P, (g + 1) * P)
                nc.tensor.matmul_mx(
                    out=acc1[:],
                    lhsT=q_codes[i][:, toks].bitcast(FP8X4),
                    lhsT_scale=q_scales[i][:, toks],
                    rhs=w1_codes[:, g, cols].bitcast(FP8X4),
                    rhs_scale=w1_scales[:, g, cols],
                    start=(g == 0),
                    stop=(g == PASSES1 - 1),
                )
            u_banks[i, h] = acc1

        def add_bias1(i):
            u = work.tile([P, D2], F32)
            row_sum = small.tile([P, HALVES1], F32)
            for h in range(HALVES1):
                cols = slice(h * BANK, (h + 1) * BANK)
                nc.vector.scalar_tensor_tensor(
                    out=u[:, cols], in0=u_banks[i, h][:], scalar=1.0, in1=a1_all[:, cols],
                    op0=ALU.mult, op1=ALU.add, accum_out=row_sum[:, h : h + 1],
                )
            u_tiles[i] = u
            stats1[i] = {"row_sum": row_sum}

        def mean1(i):
            row_sum = stats1[i]["row_sum"]
            neg_mean = small.tile([P, 1], F32)
            nc.vector.tensor_scalar(
                out=neg_mean[:], in0=row_sum[:, 0:1], scalar1=row_sum[:, 1:2], scalar2=-1.0 / D2,
                op0=ALU.add, op1=ALU.mult,
            )
            stats1[i]["neg_mean"] = neg_mean

        def deviation1(i):
            squares = work.tile([P, D2], F32)
            sq_sum = small.tile([P, 1], F32)
            nc.scalar.activation(
                out=squares[:], in_=u_tiles[i][:], func=ACT.Square,
                bias=stats1[i]["neg_mean"][:], scale=1.0, accum_out=sq_sum[:],
            )
            stats1[i]["sq_sum"] = sq_sum

        def inverse_deviation1(i):
            rstd = small.tile([P, 1], F32)
            nc.scalar.activation(
                out=rstd[:], in_=stats1[i]["sq_sum"][:], func=ACT.Abs_reciprocal_sqrt,
                bias=eps[:], scale=1.0 / D2,
            )
            stats1[i]["rstd"] = rstd

        def normalise1(i):
            z = work.tile([P, D2], F32)
            nc.vector.tensor_scalar(
                out=z[:], in0=u_tiles[i][:], scalar1=stats1[i]["neg_mean"][:], scalar2=stats1[i]["rstd"][:],
                op0=ALU.add, op1=ALU.mult,
            )
            z_tiles[i] = z

        def transpose_z(i):
            z_banks[i] = []
            for c in range(PASSES2):
                zt = psum.tile([P, PACK, P], F32)
                for t in range(PACK):
                    first = K_PASS * c + P * t
                    nc.tensor.transpose(zt[:, t, :], z_tiles[i][:, first : first + P], ident[:])
                z_banks[i].append(zt)

        def gain_shift_relu1(i):
            planes = work.tile([P, PACK, PASSES2, P], BF16)
            for c in range(PASSES2):
                for t in range(PACK):
                    j = PACK * c + t
                    nc.scalar.activation(
                        out=planes[:, t, c, :], in_=z_banks[i][c][:, t, :], func=ACT.Relu,
                        scale=gb[:, j : j + 1], bias=gb[:, D2 // P + j : D2 // P + j + 1],
                    )
            j_planes[i] = planes

        def regroup_j1(i):
            jg = work.tile([P, PASSES2 * P, PACK], BF16, align_bytes=64)
            regroup(nc.vector.tensor_copy, jg[:], j_planes[i][:].rearrange("p t c n -> p t (c n)"))
            j_grouped[i] = jg

        def quantise_j1(i):
            jc = work.tile([P, PASSES2 * P], U32, align_bytes=64)
            js = work.tile([P, PASSES2 * P], U8, align_bytes=64)
            nc.vector.quantize_mx(
                out=jc[:].bitcast(FP8X4), scales=js[:],
                in_=j_grouped[i][:].rearrange("p n t -> p (n t)"),
            )
            j_codes[i] = jc
            j_scales[i] = js

        def second_product(i):
            acc2 = psum.tile([P, BANK], F32)
            for c in range(PASSES2):
                toks = slice(c * P, (c + 1) * P)
                nc.tensor.matmul_mx(
                    out=acc2[:],
                    lhsT=j_codes[i][:, toks].bitcast(FP8X4),
                    lhsT_scale=j_scales[i][:, toks],
                    rhs=w2_codes[:, c, :].bitcast(FP8X4),
                    rhs_scale=w2_scales[:, c, :],
                    start=(c == 0),
                    stop=(c == PASSES2 - 1),
                )
            w_banks[i] = acc2

        def add_bias2(i):
            w = work.tile([P, D4], F32, bufs=3)
            row_sum2 = small.tile([P, 1], F32)
            nc.vector.scalar_tensor_tensor(
                out=w[:], in0=w_banks[i][:], scalar=1.0, in1=a2_all[:],
                op0=ALU.mult, op1=ALU.add, accum_out=row_sum2[:],
            )
            w_tiles[i] = w
            stats2[i] = {"row_sum": row_sum2}

        def mean2(i):
            neg_mean2 = small.tile([P, 1], F32)
            nc.vector.tensor_scalar(
                out=neg_mean2[:], in0=stats2[i]["row_sum"][:], scalar1=-1.0 / D4, scalar2=None,
                op0=ALU.mult,
            )
            stats2[i]["neg_mean"] = neg_mean2

        def deviation2(i):
            squares2 = work.tile([P, D4], F32)
            sq_sum2 = small.tile([P, 1], F32)
            nc.scalar.activation(
                out=squares2[:], in_=w_tiles[i][:], func=ACT.Square,
                bias=stats2[i]["neg_mean"][:], scale=1.0, accum_out=sq_sum2[:],
            )
            stats2[i]["sq_sum"] = sq_sum2

        def inverse_deviation2(i):
            rstd2 = small.tile([P, 1], F32)
            nc.scalar.activation(
                out=rstd2[:], in_=stats2[i]["sq_sum"][:], func=ACT.Abs_reciprocal_sqrt,
                bias=eps[:], scale=1.0 / D4,
            )
            stats2[i]["rstd"] = rstd2

        x_tiles = {}

        def centre_gain2(i):
            x = work.tile([P, D4], F32)
            nc.vector.scalar_tensor_tensor(
                out=x[:], in0=w_tiles[i][:], scalar=stats2[i]["neg_mean"][:], in1=g2_all[:],
                op0=ALU.add, op1=ALU.mult,
            )
            x_tiles[i] = x

        def scale_shift2(i):
            y = work.tile([P, D4], F32)
            nc.vector.scalar_tensor_tensor(
                out=y[:], in0=x_tiles[i][:], scalar=stats2[i]["rstd"][:], in1=b2_all[:],
                op0=ALU.mult, op1=ALU.add,
            )
            y_tiles[i] = y

        def relu_and_store(i):
            result = work.tile([P, D4], F32, bufs=3)
            nc.scalar.activation(out=result[:], in_=y_tiles[i][:], func=ACT.Relu)
            nc.sync.dma_start(out=out_rows[i * P : (i + 1) * P, :], in_=result[:])

        def run(step, i, *more):
            if 0 <= i < TILES:
                step(i, *more)

        def period(i):
            if Q_BUFS <= i + 1 + Q_BUFS < TILES:
                load_query(i + 1 + Q_BUFS)
            run(first_product, i, 0)
            run(transpose_query, i + 2)
            run(first_product, i, 1)
            run(transpose_z, i - 2)
            run(regroup_j1, i - 3)
            run(mean2, i - 4)
            run(quantise_query, i + 1)
            if i == W1_PERIOD:
                for g in range(PASSES1):
                    prepare_w1(g)
                quantise_w1(PASSES1 - 1, 1)
            run(quantise_j1, i - 3)
            run(centre_gain2, i - 4)
            run(second_product, i - 3)
            run(deviation1, i - 1)
            run(deviation2, i - 4)
            run(query_out_of_psum, i + 2)
            if i == W2_REGROUP_PERIOD:
                for c in range(PASSES2):
                    regroup_w2(c)
            run(inverse_deviation1, i - 1)
            run(inverse_deviation2, i - 4)
            run(gain_shift_relu1, i - 2)
            run(relu_and_store, i - 5)
            run(add_bias1, i)
            run(normalise1, i - 1)
            run(scale_shift2, i - 4)
            run(mean1, i)
            run(add_bias2, i - 3)
            if i == W2_QUANTISE_PERIOD:
                for c in range(PASSES2):
                    quantise_w2(c)

        for i in range(-2, TILES + 5):
            period(i)
